import numpy as np
import ml_dtypes

BF16 = ml_dtypes.bfloat16


def bf(x):
    return np.asarray(x, np.float32).astype(BF16)


def f32(x):
    return np.asarray(x, np.float32)


def f64(x):
    return np.asarray(x).astype(np.float64)


def striped(idx):
    return np.tile(idx.reshape(-1, 16).T, (8, 1))


S, DN, E, N, D, HEADS, HD, EMB, RUN, K = 1024, 128, 1024, 2048, 512, 4, 128, 256, 512, 4
NEG = -1e9


def gelu_tanh(v):
    return 0.5 * v * (1.0 + np.tanh(np.sqrt(2.0 / np.pi) * (v + 0.044715 * v**3)))


def setup_inputs():
    rn = np.random.standard_normal
    inputs = {}
    inputs["table"] = bf(rn((DN, S)))
    inputs["wn"] = bf(rn((DN, D)) / np.sqrt(2.0 * DN))
    inputs["edge_feats"] = f32(rn((D, E)))
    inputs["wq"] = bf(rn((D, D)) / np.sqrt(D))
    inputs["wk"] = bf(rn((D, D)) / np.sqrt(D))
    inputs["wv"] = bf(rn((D, D)) / np.sqrt(D))
    inputs["wo"] = bf(rn((D, D)) / np.sqrt(D))
    inputs["w1"] = bf(2.0 * rn((D, EMB)) / np.sqrt(D))
    inputs["b1"] = f32(0.1 * rn((EMB, 1)))
    inputs["w2"] = bf(rn((EMB, EMB)) / np.sqrt(EMB))
    inputs["b2"] = f32(0.1 * rn((EMB, 1)))
    inputs["adj"] = f32(np.maximum(np.random.random((E, E)) < 0.5, np.eye(E)))
    idx = np.concatenate([np.random.permutation(S)[:RUN] for _ in range(K)])
    inputs["offs"] = striped(idx)
    return inputs


def reference(table, wn, edge_feats, wq, wk, wv, wo, w1, b1, w2, b2, adj, offs):
    idx = offs[:16].T.reshape(-1)
    proj = f64(wn).T @ f64(table)[:, idx]
    h = f64(edge_feats) + proj[:, :E] + proj[:, E:]
    q = (f64(wq).T @ h).reshape(HEADS, HD, E)
    kk = (f64(wk).T @ h).reshape(HEADS, HD, E)
    v = (f64(wv).T @ h).reshape(HEADS, HD, E)
    scores = np.matmul(kk.transpose(0, 2, 1), q) / np.sqrt(HD)
    scores = np.where(f64(adj)[None, :, :] > 0.5, scores, NEG)
    scores = scores - scores.max(axis=1, keepdims=True)
    num = np.exp(scores)
    att = num / num.sum(axis=1, keepdims=True)
    ctx = np.matmul(v, att).reshape(D, E)
    eo = f64(wo).T @ ctx
    x = gelu_tanh(f64(w1).T @ eo + f64(b1))
    return f64(w2).T @ x + f64(b2)

@@ -1,0 +1,211 @@
+import math
+
+import concourse.mybir as mybir
+from concourse.masks import make_identity
+
+BF16 = mybir.dt.bfloat16
+F32 = mybir.dt.float32
+U16 = mybir.dt.uint16
+ALU = mybir.AluOpType
+ACT = mybir.ActivationFunctionType
+AXIS = mybir.AxisListType
+
+P = 128
+NODES = 1024
+EDGES = 1024
+LIST = 2 * EDGES
+FEAT = 512
+HEADS = 4
+EMB = 256
+BANK = 512
+BANK_OFFS = BANK // 16
+HALVES = EDGES // BANK
+BLOCKS = EDGES // P
+FEAT_BLOCKS = FEAT // P
+EMB_BLOCKS = EMB // P
+SCALE = 1.0 / math.sqrt(P)
+MASKED = -1.0e9
+
+FLOPS = 2 * (
+    P * FEAT * LIST
+    + 3 * FEAT * FEAT * EDGES
+    + 2 * FEAT * EDGES * EDGES
+    + FEAT * FEAT * EDGES
+    + FEAT * EMB * EDGES
+    + EMB * EMB * EDGES
+)
+
+
+def block(n):
+    return slice(n * P, (n + 1) * P)
+
+
+def half(n):
+    return slice(n * BANK, (n + 1) * BANK)
+
+
+def accumulate(nc, acc, pairs):
+    for n, (lhsT, rhs) in enumerate(pairs):
+        nc.tensor.matmul(acc, lhsT, rhs, start=(n == 0), stop=(n == len(pairs) - 1))
+
+
+def tile_edgeencoder_b_kernel(
+    tc, table, wn, edge_feats, wq, wk, wv, wo, w1, b1, w2, b2, adj, offs, out
+):
+    nc = tc.nc
+    with (
+        tc.tile_pool(name="held", bufs=1) as held,
+        tc.tile_pool(name="stage", bufs=3) as stage,
+        tc.tile_pool(name="work", bufs=3) as work,
+        tc.tile_pool(name="stats", bufs=4) as stats,
+        tc.tile_pool(name="flip", bufs=2) as flip,
+        tc.psum_pool(name="psum_s", bufs=4) as psum_s,
+        tc.psum_pool(name="psum_t", bufs=2) as psum_t,
+        tc.psum_pool(name="psum_a", bufs=2) as psum_a,
+    ):
+        offsets = held.tile([P, LIST // 16], U16, name="offsets")
+        nc.sync.dma_start(offsets[:], offs)
+        nodes = held.tile([P, NODES], BF16, name="nodes")
+        nc.sync.dma_start(nodes[:], table)
+        wn_sb = held.tile([P, FEAT], BF16, name="wn_sb")
+        nc.sync.dma_start(wn_sb[:], wn)
+        feats = held.tile([P, FEAT_BLOCKS, EDGES], F32, name="feats")
+        for m in range(FEAT_BLOCKS):
+            nc.scalar.dma_start(feats[:, m, :], edge_feats[block(m), :])
+
+        def load_weights(queue, name, w, columns):
+            w_sb = held.tile([P, w.shape[0] // P, columns], BF16, name=name)
+            queue.dma_start(w_sb[:], w.rearrange("(c p) m -> p c m", p=P))
+            return w_sb
+
+        wk_sb = load_weights(nc.sync, "wk_sb", wk, FEAT)
+        wq_sb = load_weights(nc.sync, "wq_sb", wq, FEAT)
+        adj_blocks = []
+        for k in range(BLOCKS):
+            adj_k = stage.tile([P, EDGES], F32, name="adj_k", bufs=BLOCKS)
+            nc.sync.dma_start(adj_k[:], adj[block(k), :])
+            adj_blocks.append(adj_k)
+        wv_sb = load_weights(nc.scalar, "wv_sb", wv, FEAT)
+        wo_sb = load_weights(nc.scalar, "wo_sb", wo, FEAT)
+        w1_sb = load_weights(nc.scalar, "w1_sb", w1, EMB)
+        w2_sb = load_weights(nc.scalar, "w2_sb", w2, EMB)
+        bias_row = held.tile([1, 2 * EMB], F32, name="bias_row")
+        nc.scalar.dma_start(bias_row[:, 0:EMB], b1.rearrange("r o -> o r"))
+        nc.scalar.dma_start(bias_row[:, EMB : 2 * EMB], b2.rearrange("r o -> o r"))
+
+        ident = held.tile([P, P], BF16, name="ident")
+        make_identity(nc, ident[:])
+        one = held.tile([1, 1], F32, name="one")
+        nc.vector.memset(one[:], 1.0)
+
+        h = held.tile([P, FEAT_BLOCKS, EDGES], BF16, name="h")
+        for m in range(FEAT_BLOCKS):
+            for j in range(HALVES):
+                acc = psum_a.tile([P, BANK], F32, name="acc")
+                for end in range(2):
+                    piece = end * HALVES + j
+                    nc.tensor.matmul(
+                        acc[:],
+                        wn_sb[:, block(m)],
+                        nodes[:].indirect(offsets[:, piece * BANK_OFFS : (piece + 1) * BANK_OFFS]),
+                        start=(end == 0),
+                        stop=(end == 1),
+                    )
+                nc.vector.tensor_tensor(h[:, m, half(j)], acc[:], feats[:, m, half(j)], ALU.add)
+
+        bias_ps = psum_a.tile([P, 2 * EMB_BLOCKS], F32, name="acc")
+        for n in range(2 * EMB_BLOCKS):
+            nc.tensor.matmul(bias_ps[:, n : n + 1], bias_row[:, block(n)], one[:], start=True, stop=True)
+        bias = held.tile([P, 2 * EMB_BLOCKS], F32, name="bias")
+        nc.vector.tensor_copy(bias[:], bias_ps[:])
+
+        mask_t = held.tile([P, BLOCKS, EDGES], BF16, name="mask_t")
+        for k in range(BLOCKS):
+            mask_k = stage.tile([P, EDGES], BF16, name="mask_k")
+            nc.gpsimd.tensor_scalar(mask_k[:], adj_blocks[k][:], -1.0, -MASKED, ALU.add, ALU.mult)
+            flipped = psum_t.tile([P, BLOCKS, P], BF16, name="flipped")
+            for i in range(BLOCKS):
+                nc.tensor.transpose(flipped[:, i, :], mask_k[:, block(i)], ident[:])
+            nc.scalar.copy(mask_t[:, :, block(k)], flipped[:])
+
+        q = held.tile([P, HEADS, EDGES], BF16, name="q")
+        kk = held.tile([P, HEADS, EDGES], BF16, name="kk")
+        v_t = held.tile([P, BLOCKS, FEAT], BF16, name="v_t")
+        ctx = held.tile([P, HEADS, EDGES], BF16, name="ctx")
+        eo = held.tile([P, FEAT_BLOCKS, EDGES], BF16, name="eo")
+        x = held.tile([P, EMB_BLOCKS, EDGES], BF16, name="x")
+        y = held.tile([P, EMB_BLOCKS, EDGES], F32, name="y")
+
+        def project(w_sb, a, dest):
+            for j in range(HALVES):
+                acc = psum_a.tile([P, BANK], F32, name="acc")
+                accumulate(
+                    nc, acc[:], [(w_sb[:, c, block(a)], h[:, c, half(j)]) for c in range(FEAT_BLOCKS)]
+                )
+                nc.scalar.copy(dest[:, a, half(j)], acc[:])
+
+        def values():
+            for k in range(BLOCKS):
+                acc = psum_a.tile([P, BANK], F32, name="acc")
+                accumulate(
+                    nc, acc[:], [(h[:, c, block(k)], wv_sb[:, c, :]) for c in range(FEAT_BLOCKS)]
+                )
+                nc.scalar.copy(v_t[:, k, :], acc[:])
+
+        def attend(a, i, att_t, b):
+            z = work.tile([P, EDGES], F32, name="z")
+            for n in range(HALVES):
+                s = psum_s.tile([P, BANK], F32, name="s")
+                nc.tensor.matmul(s[:], q[:, a, block(i)], kk[:, a, half(n)], start=True, stop=True)
+                nc.vector.scalar_tensor_tensor(
+                    z[:, half(n)], s[:], SCALE, mask_t[:, i, half(n)], ALU.mult, ALU.add
+                )
+            neg_max = stats.tile([P, 1], F32, name="neg_max")
+            nc.vector.tensor_reduce(neg_max[:], z[:], AXIS.X, ALU.max, negate=True)
+            num = work.tile([P, EDGES], F32, name="num")
+            den = stats.tile([P, 1], F32, name="den")
+            nc.scalar.activation(num[:], z[:], ACT.Exp, bias=neg_max[:], accum_out=den[:])
+            rden = stats.tile([P, 1], F32, name="rden")
+            nc.vector.reciprocal(rden[:], den[:])
+            att = work.tile([P, EDGES], BF16, name="att")
+            nc.gpsimd.tensor_scalar(att[:], num[:], rden[:], 0.0, ALU.mult, ALU.add)
+            flipped = psum_t.tile([P, BLOCKS, P], BF16, name="flipped")
+            for k in range(BLOCKS):
+                nc.tensor.transpose(flipped[:, k, :], att[:, block(k)], ident[:])
+            nc.scalar.copy(att_t[:, :, block(b)], flipped[:])
+
+        def mlp(j):
+            for m in range(FEAT_BLOCKS):
+                acc = psum_a.tile([P, BANK], F32, name="acc")
+                accumulate(nc, acc[:], [(wo_sb[:, a, block(m)], ctx[:, a, half(j)]) for a in range(HEADS)])
+                nc.scalar.copy(eo[:, m, half(j)], acc[:])
+            for r in range(EMB_BLOCKS):
+                acc = psum_a.tile([P, BANK], F32, name="acc")
+                accumulate(
+                    nc, acc[:], [(w1_sb[:, c, block(r)], eo[:, c, half(j)]) for c in range(FEAT_BLOCKS)]
+                )
+                nc.scalar.activation(x[:, r, half(j)], acc[:], ACT.Gelu_apprx_tanh, bias=bias[:, r : r + 1])
+            for r in range(EMB_BLOCKS):
+                acc = psum_a.tile([P, BANK], F32, name="acc")
+                accumulate(
+                    nc, acc[:], [(w2_sb[:, c, block(r)], x[:, c, half(j)]) for c in range(EMB_BLOCKS)]
+                )
+                nc.vector.tensor_scalar_add(
+                    y[:, r, half(j)], acc[:], bias[:, EMB_BLOCKS + r : EMB_BLOCKS + r + 1]
+                )
+                nc.sync.dma_start(out[block(r), half(j)], y[:, r, half(j)])
+
+        for j in range(HALVES):
+            for a in range(HEADS):
+                if j == 0:
+                    project(wk_sb, a, kk)
+                    project(wq_sb, a, q)
+                att_t = flip.tile([P, BLOCKS, BANK], BF16, name="att_t")
+                for b in range(BANK // P):
+                    attend(a, j * (BANK // P) + b, att_t, b)
+                if j == 0 and a == 0:
+                    values()
+                acc = psum_a.tile([P, BANK], F32, name="acc")
+                accumulate(nc, acc[:], [(v_t[:, k, block(a)], att_t[:, k, :]) for k in range(BLOCKS)])
+                nc.scalar.copy(ctx[:, a, half(j)], acc[:])
+            mlp(j)

@@ -19,6 +19,7 @@ HEADS = 4
 EMB = 256
 BANK = 512
 BANK_OFFS = BANK // 16
+BANK_BLOCKS = BANK // P
 HALVES = EDGES // BANK
 BLOCKS = EDGES // P
 FEAT_BLOCKS = FEAT // P
@@ -44,9 +45,9 @@ def half(n):
     return slice(n * BANK, (n + 1) * BANK)
 
 
-def accumulate(nc, acc, pairs):
+def accumulate(nc, acc, pairs, start=True, stop=True):
     for n, (lhsT, rhs) in enumerate(pairs):
-        nc.tensor.matmul(acc, lhsT, rhs, start=(n == 0), stop=(n == len(pairs) - 1))
+        nc.tensor.matmul(acc, lhsT, rhs, start=(start and n == 0), stop=(stop and n == len(pairs) - 1))
 
 
 def tile_edgeencoder_b_kernel(
@@ -55,43 +56,43 @@ def tile_edgeencoder_b_kernel(
     nc = tc.nc
     with (
         tc.tile_pool(name="held", bufs=1) as held,
-        tc.tile_pool(name="stage", bufs=3) as stage,
+        tc.tile_pool(name="short", bufs=2) as short,
         tc.tile_pool(name="work", bufs=3) as work,
         tc.tile_pool(name="stats", bufs=4) as stats,
-        tc.tile_pool(name="flip", bufs=2) as flip,
-        tc.psum_pool(name="psum_s", bufs=4) as psum_s,
+        tc.psum_pool(name="psum_s", bufs=3) as psum_s,
         tc.psum_pool(name="psum_t", bufs=2) as psum_t,
         tc.psum_pool(name="psum_a", bufs=2) as psum_a,
+        tc.psum_pool(name="psum_c", bufs=1) as psum_c,
     ):
         offsets = held.tile([P, LIST // 16], U16, name="offsets")
         nc.sync.dma_start(offsets[:], offs)
+
         nodes = held.tile([P, NODES], BF16, name="nodes")
-        nc.sync.dma_start(nodes[:], table)
         wn_sb = held.tile([P, FEAT], BF16, name="wn_sb")
-        nc.sync.dma_start(wn_sb[:], wn)
         feats = held.tile([P, FEAT_BLOCKS, EDGES], F32, name="feats")
-        for m in range(FEAT_BLOCKS):
-            nc.scalar.dma_start(feats[:, m, :], edge_feats[block(m), :])
-
-        def load_weights(queue, name, w, columns):
-            w_sb = held.tile([P, w.shape[0] // P, columns], BF16, name=name)
-            queue.dma_start(w_sb[:], w.rearrange("(c p) m -> p c m", p=P))
-            return w_sb
-
-        wk_sb = load_weights(nc.sync, "wk_sb", wk, FEAT)
-        wq_sb = load_weights(nc.sync, "wq_sb", wq, FEAT)
-        adj_blocks = []
-        for k in range(BLOCKS):
-            adj_k = stage.tile([P, EDGES], F32, name="adj_k", bufs=BLOCKS)
-            nc.sync.dma_start(adj_k[:], adj[block(k), :])
-            adj_blocks.append(adj_k)
-        wv_sb = load_weights(nc.scalar, "wv_sb", wv, FEAT)
-        wo_sb = load_weights(nc.scalar, "wo_sb", wo, FEAT)
-        w1_sb = load_weights(nc.scalar, "w1_sb", w1, EMB)
-        w2_sb = load_weights(nc.scalar, "w2_sb", w2, EMB)
+        wk_sb = held.tile([P, FEAT_BLOCKS, FEAT], BF16, name="wk_sb")
+        wq_sb = held.tile([P, FEAT_BLOCKS, FEAT], BF16, name="wq_sb")
+        wv_sb = held.tile([P, FEAT_BLOCKS, FEAT], BF16, name="wv_sb")
+        wo_sb = held.tile([P, FEAT_BLOCKS, FEAT], BF16, name="wo_sb")
+        w1_sb = held.tile([P, FEAT_BLOCKS, EMB], BF16, name="w1_sb")
+        w2_sb = held.tile([P, EMB_BLOCKS, EMB], BF16, name="w2_sb")
         bias_row = held.tile([1, 2 * EMB], F32, name="bias_row")
-        nc.scalar.dma_start(bias_row[:, 0:EMB], b1.rearrange("r o -> o r"))
-        nc.scalar.dma_start(bias_row[:, EMB : 2 * EMB], b2.rearrange("r o -> o r"))
+        adj_sb = held.tile([P, BLOCKS, BLOCKS, P], F32, name="adj_sb")
+        adj_by_key_block = adj.rearrange("(k p) e -> p k e", p=P)
+
+        def rows_in_blocks(w):
+            return w.rearrange("(c p) m -> p c m", p=P)
+
+        loads = [(nodes[:], table), (wn_sb[:], wn)]
+        loads += [(feats[:, m, :], edge_feats[block(m), :]) for m in range(FEAT_BLOCKS)]
+        loads += [(wk_sb[:], rows_in_blocks(wk)), (wq_sb[:], rows_in_blocks(wq))]
+        loads += [(adj_sb[:, i, :, :], adj_by_key_block[:, :, block(i)]) for i in range(2)]
+        loads += [(wv_sb[:], rows_in_blocks(wv))]
+        loads += [(adj_sb[:, i, :, :], adj_by_key_block[:, :, block(i)]) for i in range(2, BLOCKS)]
+        loads += [(wo_sb[:], rows_in_blocks(wo)), (w1_sb[:], rows_in_blocks(w1)), (w2_sb[:], rows_in_blocks(w2))]
+        loads += [(bias_row[:, 0:EMB], b1.rearrange("r o -> o r")), (bias_row[:, EMB : 2 * EMB], b2.rearrange("r o -> o r"))]
+        for n, (sbuf_side, dram_side) in enumerate(loads):
+            (nc.scalar, nc.sync)[n % 2].dma_start(sbuf_side, dram_side)
 
         ident = held.tile([P, P], BF16, name="ident")
         make_identity(nc, ident[:])
@@ -113,99 +114,142 @@ def tile_edgeencoder_b_kernel(
                     )
                 nc.vector.tensor_tensor(h[:, m, half(j)], acc[:], feats[:, m, half(j)], ALU.add)
 
+        q = held.tile([P, HEADS, EDGES], BF16, name="q")
+        kk = held.tile([P, HEADS, EDGES], BF16, name="kk")
+        v_t = held.tile([P, HEADS, EDGES], BF16, name="v_t")
+        mask = held.tile([P, BLOCKS, BLOCKS, P], BF16, name="mask")
+        mask_t = held.tile([P, BLOCKS, EDGES], BF16, name="mask_t")
+        ctx = held.tile([P, HEADS, EDGES], BF16, name="ctx")
+        eo = held.tile([P, FEAT_BLOCKS, EDGES], BF16, name="eo")
+        x = held.tile([P, EMB_BLOCKS, EDGES], BF16, name="x")
+        y = held.tile([P, EMB_BLOCKS, EDGES], F32, name="y")
+
+        def prepare(a, part):
+            j = part % HALVES
+            acc = psum_a.tile([P, BANK], F32, name="acc")
+            if part < 2 * HALVES:
+                w_sb, dest = ((wk_sb, kk), (wq_sb, q))[part // HALVES]
+                accumulate(nc, acc[:], [(w_sb[:, c, block(a)], h[:, c, half(j)]) for c in range(FEAT_BLOCKS)])
+                nc.vector.tensor_copy(dest[:, a, half(j)], acc[:])
+            else:
+                for n in range(BANK_BLOCKS):
+                    k = j * BANK_BLOCKS + n
+                    accumulate(nc, acc[:, block(n)], [(h[:, c, block(k)], wv_sb[:, c, block(a)]) for c in range(FEAT_BLOCKS)])
+                nc.scalar.copy(v_t[:, a, half(j)], acc[:])
+
+        def flip_mask(i):
+            flipped = psum_t.tile([P, EDGES], BF16, name="flipped")
+            for k in range(BLOCKS):
+                nc.tensor.transpose(flipped[:, block(k)], mask[:, i, k, :], ident[:])
+            nc.vector.tensor_copy(mask_t[:, i, :], flipped[:])
+
+        blocks = [(a, i) for a in range(HEADS) for i in range(BLOCKS)]
+        s_of, z_of, num_of, den_of, att_of = {}, {}, {}, {}, {}
+        att_t_of, ctx_of = {}, {}
+
+        def scores(n):
+            a, i = blocks[n]
+            s_of[n] = []
+            for t in range(HALVES):
+                s = psum_s.tile([P, BANK], F32, name="s")
+                nc.tensor.matmul(s[:], q[:, a, block(i)], kk[:, a, half(t)], start=True, stop=True)
+                s_of[n].append(s)
+
+        def scale_and_mask(n):
+            i = blocks[n][1]
+            z_of[n] = short.tile([P, EDGES], F32, name="z")
+            for t in range(HALVES):
+                nc.vector.scalar_tensor_tensor(
+                    z_of[n][:, half(t)], s_of[n][t][:], SCALE, mask_t[:, i, half(t)], ALU.mult, ALU.add
+                )
+
+        def exponentials(n):
+            neg_max = stats.tile([P, 1], F32, name="neg_max")
+            nc.vector.tensor_reduce(neg_max[:], z_of[n][:], AXIS.X, ALU.max, negate=True)
+            num_of[n] = work.tile([P, EDGES], F32, name="num")
+            den_of[n] = stats.tile([P, 1], F32, name="den")
+            nc.scalar.activation(num_of[n][:], z_of[n][:], ACT.Exp, bias=neg_max[:], accum_out=den_of[n][:])
+
+        def divide(n):
+            rden = stats.tile([P, 1], F32, name="rden")
+            nc.vector.reciprocal(rden[:], den_of[n][:])
+            att_of[n] = work.tile([P, EDGES], BF16, name="att")
+            nc.gpsimd.tensor_scalar(att_of[n][:], num_of[n][:], rden[:], 0.0, ALU.mult, ALU.add)
+
+        def flip_weights(n):
+            group, b = divmod(n, BANK_BLOCKS)
+            if b == 0:
+                att_t_of[group] = work.tile([P, BLOCKS, BANK], BF16, name="att_t")
+            flipped = psum_t.tile([P, EDGES], BF16, name="flipped")
+            for k in range(BLOCKS):
+                nc.tensor.transpose(flipped[:, block(k)], att_of[n][:, block(k)], ident[:])
+            nc.scalar.copy(att_t_of[group][:, :, block(b)], flipped[:].rearrange("p (k e) -> p k e", k=BLOCKS))
+
+        def context(group, part):
+            a, j = divmod(group, HALVES)
+            if part == 0:
+                ctx_of[group] = psum_c.tile([P, BANK], F32, name="ctx_ps")
+            keys = range(2 * part, 2 * part + 2)
+            accumulate(
+                nc,
+                ctx_of[group][:],
+                [(v_t[:, a, block(k)], att_t_of[group][:, k, :]) for k in keys],
+                start=(part == 0),
+                stop=(part == 3),
+            )
+            if part == 3:
+                nc.scalar.copy(ctx[:, a, half(j)], ctx_of[group][:])
+
+        for i in range(BLOCKS):
+            nc.gpsimd.tensor_scalar(mask[:, i, :, :], adj_sb[:, i, :, :], -1.0, -MASKED, ALU.add, ALU.mult)
+        products = [(a, part) for a in range(HEADS) for part in range(6)]
+        for a, part in products[:3]:
+            prepare(a, part)
+        flip_mask(0)
+        scores(0)
+        flip_mask(1)
+
+        for n in range(len(blocks) + 6):
+            if n < len(blocks):
+                scale_and_mask(n)
+            if n + 1 < len(blocks):
+                scores(n + 1)
+            if n < len(blocks):
+                exponentials(n)
+            if 0 <= n - 1 < len(blocks):
+                divide(n - 1)
+            if n + 2 < BLOCKS:
+                flip_mask(n + 2)
+            m = 3 + 3 * (n // 4) + n % 4
+            if n % 4 != 3 and m < len(products):
+                prepare(*products[m])
+            if n >= 6:
+                context(*divmod(n - 6, 4))
+            if 0 <= n - 2 < len(blocks):
+                flip_weights(n - 2)
+
         bias_ps = psum_a.tile([P, 2 * EMB_BLOCKS], F32, name="acc")
         for n in range(2 * EMB_BLOCKS):
             nc.tensor.matmul(bias_ps[:, n : n + 1], bias_row[:, block(n)], one[:], start=True, stop=True)
         bias = held.tile([P, 2 * EMB_BLOCKS], F32, name="bias")
         nc.vector.tensor_copy(bias[:], bias_ps[:])
 
-        mask_t = held.tile([P, BLOCKS, EDGES], BF16, name="mask_t")
-        for k in range(BLOCKS):
-            mask_k = stage.tile([P, EDGES], BF16, name="mask_k")
-            nc.gpsimd.tensor_scalar(mask_k[:], adj_blocks[k][:], -1.0, -MASKED, ALU.add, ALU.mult)
-            flipped = psum_t.tile([P, BLOCKS, P], BF16, name="flipped")
-            for i in range(BLOCKS):
-                nc.tensor.transpose(flipped[:, i, :], mask_k[:, block(i)], ident[:])
-            nc.scalar.copy(mask_t[:, :, block(k)], flipped[:])
-
-        q = held.tile([P, HEADS, EDGES], BF16, name="q")
-        kk = held.tile([P, HEADS, EDGES], BF16, name="kk")
-        v_t = held.tile([P, BLOCKS, FEAT], BF16, name="v_t")
-        ctx = held.tile([P, HEADS, EDGES], BF16, name="ctx")
-        eo = held.tile([P, FEAT_BLOCKS, EDGES], BF16, name="eo")
-        x = held.tile([P, EMB_BLOCKS, EDGES], BF16, name="x")
-        y = held.tile([P, EMB_BLOCKS, EDGES], F32, name="y")
-
-        def project(w_sb, a, dest):
+        for m in range(FEAT_BLOCKS):
             for j in range(HALVES):
                 acc = psum_a.tile([P, BANK], F32, name="acc")
-                accumulate(
-                    nc, acc[:], [(w_sb[:, c, block(a)], h[:, c, half(j)]) for c in range(FEAT_BLOCKS)]
-                )
-                nc.scalar.copy(dest[:, a, half(j)], acc[:])
-
-        def values():
-            for k in range(BLOCKS):
-                acc = psum_a.tile([P, BANK], F32, name="acc")
-                accumulate(
-                    nc, acc[:], [(h[:, c, block(k)], wv_sb[:, c, :]) for c in range(FEAT_BLOCKS)]
-                )
-                nc.scalar.copy(v_t[:, k, :], acc[:])
-
-        def attend(a, i, att_t, b):
-            z = work.tile([P, EDGES], F32, name="z")
-            for n in range(HALVES):
-                s = psum_s.tile([P, BANK], F32, name="s")
-                nc.tensor.matmul(s[:], q[:, a, block(i)], kk[:, a, half(n)], start=True, stop=True)
-                nc.vector.scalar_tensor_tensor(
-                    z[:, half(n)], s[:], SCALE, mask_t[:, i, half(n)], ALU.mult, ALU.add
-                )
-            neg_max = stats.tile([P, 1], F32, name="neg_max")
-            nc.vector.tensor_reduce(neg_max[:], z[:], AXIS.X, ALU.max, negate=True)
-            num = work.tile([P, EDGES], F32, name="num")
-            den = stats.tile([P, 1], F32, name="den")
-            nc.scalar.activation(num[:], z[:], ACT.Exp, bias=neg_max[:], accum_out=den[:])
-            rden = stats.tile([P, 1], F32, name="rden")
-            nc.vector.reciprocal(rden[:], den[:])
-            att = work.tile([P, EDGES], BF16, name="att")
-            nc.gpsimd.tensor_scalar(att[:], num[:], rden[:], 0.0, ALU.mult, ALU.add)
-            flipped = psum_t.tile([P, BLOCKS, P], BF16, name="flipped")
-            for k in range(BLOCKS):
-                nc.tensor.transpose(flipped[:, k, :], att[:, block(k)], ident[:])
-            nc.scalar.copy(att_t[:, :, block(b)], flipped[:])
-
-        def mlp(j):
-            for m in range(FEAT_BLOCKS):
-                acc = psum_a.tile([P, BANK], F32, name="acc")
                 accumulate(nc, acc[:], [(wo_sb[:, a, block(m)], ctx[:, a, half(j)]) for a in range(HEADS)])
-                nc.scalar.copy(eo[:, m, half(j)], acc[:])
-            for r in range(EMB_BLOCKS):
-                acc = psum_a.tile([P, BANK], F32, name="acc")
-                accumulate(
-                    nc, acc[:], [(w1_sb[:, c, block(r)], eo[:, c, half(j)]) for c in range(FEAT_BLOCKS)]
-                )
-                nc.scalar.activation(x[:, r, half(j)], acc[:], ACT.Gelu_apprx_tanh, bias=bias[:, r : r + 1])
-            for r in range(EMB_BLOCKS):
-                acc = psum_a.tile([P, BANK], F32, name="acc")
-                accumulate(
-                    nc, acc[:], [(w2_sb[:, c, block(r)], x[:, c, half(j)]) for c in range(EMB_BLOCKS)]
-                )
-                nc.vector.tensor_scalar_add(
-                    y[:, r, half(j)], acc[:], bias[:, EMB_BLOCKS + r : EMB_BLOCKS + r + 1]
-                )
-                nc.sync.dma_start(out[block(r), half(j)], y[:, r, half(j)])
-
-        for j in range(HALVES):
-            for a in range(HEADS):
                 if j == 0:
-                    project(wk_sb, a, kk)
-                    project(wq_sb, a, q)
-                att_t = flip.tile([P, BLOCKS, BANK], BF16, name="att_t")
-                for b in range(BANK // P):
-                    attend(a, j * (BANK // P) + b, att_t, b)
-                if j == 0 and a == 0:
-                    values()
+                    nc.scalar.copy(eo[:, m, half(j)], acc[:])
+                else:
+                    nc.vector.tensor_copy(eo[:, m, half(j)], acc[:])
+        for r in range(EMB_BLOCKS):
+            for j in range(HALVES):
                 acc = psum_a.tile([P, BANK], F32, name="acc")
-                accumulate(nc, acc[:], [(v_t[:, k, block(a)], att_t[:, k, :]) for k in range(BLOCKS)])
-                nc.scalar.copy(ctx[:, a, half(j)], acc[:])
-            mlp(j)
+                accumulate(nc, acc[:], [(w1_sb[:, c, block(r)], eo[:, c, half(j)]) for c in range(FEAT_BLOCKS)])
+                nc.scalar.activation(x[:, r, half(j)], acc[:], ACT.Gelu_apprx_tanh, bias=bias[:, r : r + 1])
+        for r in range(EMB_BLOCKS):
+            for j in range(HALVES):
+                acc = psum_a.tile([P, BANK], F32, name="acc")
+                accumulate(nc, acc[:], [(w2_sb[:, c, block(r)], x[:, c, half(j)]) for c in range(EMB_BLOCKS)])
+                nc.vector.tensor_scalar_add(y[:, r, half(j)], acc[:], bias[:, EMB_BLOCKS + r : EMB_BLOCKS + r + 1])
+                nc.sync.dma_start(out[block(r), half(j)], y[:, r, half(j)])

@@ -143,7 +143,8 @@ def tile_edgeencoder_b_kernel(
                 nc.tensor.transpose(flipped[:, block(k)], mask[:, i, k, :], ident[:])
             nc.vector.tensor_copy(mask_t[:, i, :], flipped[:])
 
-        blocks = [(a, i) for a in range(HEADS) for i in range(BLOCKS)]
+        groups = [(0, 0), (0, 1), (1, 0), (1, 1), (2, 0), (3, 0), (2, 1), (3, 1)]
+        blocks = [(a, j * BANK_BLOCKS + b) for a, j in groups for b in range(BANK_BLOCKS)]
         s_of, z_of, num_of, den_of, att_of = {}, {}, {}, {}, {}
         att_t_of, ctx_of = {}, {}
 
@@ -186,19 +187,38 @@ def tile_edgeencoder_b_kernel(
             nc.scalar.copy(att_t_of[group][:, :, block(b)], flipped[:].rearrange("p (k e) -> p k e", k=BLOCKS))
 
         def context(group, part):
-            a, j = divmod(group, HALVES)
+            a, j = groups[group]
             if part == 0:
                 ctx_of[group] = psum_c.tile([P, BANK], F32, name="ctx_ps")
-            keys = range(2 * part, 2 * part + 2)
+            keys = range(part * BANK_BLOCKS, (part + 1) * BANK_BLOCKS)
             accumulate(
                 nc,
                 ctx_of[group][:],
                 [(v_t[:, a, block(k)], att_t_of[group][:, k, :]) for k in keys],
                 start=(part == 0),
-                stop=(part == 3),
+                stop=(part == 1),
             )
-            if part == 3:
+            if part == 1:
                 nc.scalar.copy(ctx[:, a, half(j)], ctx_of[group][:])
+
+        def edge_out(j, m):
+            acc = psum_a.tile([P, BANK], F32, name="acc")
+            accumulate(nc, acc[:], [(wo_sb[:, a, block(m)], ctx[:, a, half(j)]) for a in range(HEADS)])
+            if m % 2 == 0:
+                nc.scalar.copy(eo[:, m, half(j)], acc[:])
+            else:
+                nc.vector.tensor_copy(eo[:, m, half(j)], acc[:])
+
+        def hidden(j, r):
+            acc = psum_a.tile([P, BANK], F32, name="acc")
+            accumulate(nc, acc[:], [(w1_sb[:, c, block(r)], eo[:, c, half(j)]) for c in range(FEAT_BLOCKS)])
+            nc.scalar.activation(x[:, r, half(j)], acc[:], ACT.Gelu_apprx_tanh, bias=bias[:, r : r + 1])
+
+        def embed(j, r):
+            acc = psum_a.tile([P, BANK], F32, name="acc")
+            accumulate(nc, acc[:], [(w2_sb[:, c, block(r)], x[:, c, half(j)]) for c in range(EMB_BLOCKS)])
+            nc.vector.tensor_scalar_add(y[:, r, half(j)], acc[:], bias[:, EMB_BLOCKS + r : EMB_BLOCKS + r + 1])
+            nc.sync.dma_start(out[block(r), half(j)], y[:, r, half(j)])
 
         for i in range(BLOCKS):
             nc.gpsimd.tensor_scalar(mask[:, i, :, :], adj_sb[:, i, :, :], -1.0, -MASKED, ALU.add, ALU.mult)
@@ -209,24 +229,27 @@ def tile_edgeencoder_b_kernel(
         scores(0)
         flip_mask(1)
 
-        for n in range(len(blocks) + 6):
-            if n < len(blocks):
-                scale_and_mask(n)
+        for n in range(len(blocks)):
+            scale_and_mask(n)
             if n + 1 < len(blocks):
                 scores(n + 1)
-            if n < len(blocks):
-                exponentials(n)
-            if 0 <= n - 1 < len(blocks):
+            exponentials(n)
+            if n >= 1:
                 divide(n - 1)
             if n + 2 < BLOCKS:
                 flip_mask(n + 2)
-            m = 3 + 3 * (n // 4) + n % 4
-            if n % 4 != 3 and m < len(products):
-                prepare(*products[m])
-            if n >= 6:
-                context(*divmod(n - 6, 4))
-            if 0 <= n - 2 < len(blocks):
+            if n + 3 < len(products):
+                prepare(*products[n + 3])
+            if n >= 6 and (n - 6) % 4 < 2:
+                context((n - 6) // 4, (n - 6) % 4)
+            if n >= 28:
+                edge_out(0, n - 28)
+            if n >= 2:
                 flip_weights(n - 2)
+
+        divide(len(blocks) - 1)
+        flip_weights(len(blocks) - 2)
+        flip_weights(len(blocks) - 1)
 
         bias_ps = psum_a.tile([P, 2 * EMB_BLOCKS], F32, name="acc")
         for n in range(2 * EMB_BLOCKS):
@@ -234,22 +257,15 @@ def tile_edgeencoder_b_kernel(
         bias = held.tile([P, 2 * EMB_BLOCKS], F32, name="bias")
         nc.vector.tensor_copy(bias[:], bias_ps[:])
 
+        for r in range(EMB_BLOCKS):
+            hidden(0, r)
+        for part in range(2):
+            context(len(groups) - 1, part)
+        for r in range(EMB_BLOCKS):
+            embed(0, r)
         for m in range(FEAT_BLOCKS):
-            for j in range(HALVES):
-                acc = psum_a.tile([P, BANK], F32, name="acc")
-                accumulate(nc, acc[:], [(wo_sb[:, a, block(m)], ctx[:, a, half(j)]) for a in range(HEADS)])
-                if j == 0:
-                    nc.scalar.copy(eo[:, m, half(j)], acc[:])
-                else:
-                    nc.vector.tensor_copy(eo[:, m, half(j)], acc[:])
+            edge_out(1, m)
         for r in range(EMB_BLOCKS):
-            for j in range(HALVES):
-                acc = psum_a.tile([P, BANK], F32, name="acc")
-                accumulate(nc, acc[:], [(w1_sb[:, c, block(r)], eo[:, c, half(j)]) for c in range(FEAT_BLOCKS)])
-                nc.scalar.activation(x[:, r, half(j)], acc[:], ACT.Gelu_apprx_tanh, bias=bias[:, r : r + 1])
+            hidden(1, r)
         for r in range(EMB_BLOCKS):
-            for j in range(HALVES):
-                acc = psum_a.tile([P, BANK], F32, name="acc")
-                accumulate(nc, acc[:], [(w2_sb[:, c, block(r)], x[:, c, half(j)]) for c in range(EMB_BLOCKS)])
-                nc.vector.tensor_scalar_add(y[:, r, half(j)], acc[:], bias[:, EMB_BLOCKS + r : EMB_BLOCKS + r + 1])
-                nc.sync.dma_start(out[block(r), half(j)], y[:, r, half(j)])
+            embed(1, r)

@@ -125,17 +125,17 @@ def tile_edgeencoder_b_kernel(
         y = held.tile([P, EMB_BLOCKS, EDGES], F32, name="y")
 
         def prepare(a, part):
-            j = part % HALVES
             acc = psum_a.tile([P, BANK], F32, name="acc")
-            if part < 2 * HALVES:
-                w_sb, dest = ((wk_sb, kk), (wq_sb, q))[part // HALVES]
+            if part in (3, 4):
+                j = part - 3
+                for b in range(BANK_BLOCKS):
+                    k = j * BANK_BLOCKS + b
+                    accumulate(nc, acc[:, block(b)], [(h[:, c, block(k)], wv_sb[:, c, block(a)]) for c in range(FEAT_BLOCKS)])
+                nc.scalar.copy(v_t[:, a, half(j)], acc[:])
+            else:
+                w_sb, dest, j = {0: (wk_sb, kk, 0), 1: (wk_sb, kk, 1), 2: (wq_sb, q, 0), 5: (wq_sb, q, 1)}[part]
                 accumulate(nc, acc[:], [(w_sb[:, c, block(a)], h[:, c, half(j)]) for c in range(FEAT_BLOCKS)])
                 nc.vector.tensor_copy(dest[:, a, half(j)], acc[:])
-            else:
-                for n in range(BANK_BLOCKS):
-                    k = j * BANK_BLOCKS + n
-                    accumulate(nc, acc[:, block(n)], [(h[:, c, block(k)], wv_sb[:, c, block(a)]) for c in range(FEAT_BLOCKS)])
-                nc.scalar.copy(v_t[:, a, half(j)], acc[:])
 
         def flip_mask(i):
             flipped = psum_t.tile([P, EDGES], BF16, name="flipped")
@@ -222,7 +222,8 @@ def tile_edgeencoder_b_kernel(
 
         for i in range(BLOCKS):
             nc.gpsimd.tensor_scalar(mask[:, i, :, :], adj_sb[:, i, :, :], -1.0, -MASKED, ALU.add, ALU.mult)
-        products = [(a, part) for a in range(HEADS) for part in range(6)]
+        products = [(a, part) for a in (0, 1) for part in range(6)]
+        products += [(a, part) for parts in (range(3), range(3, 6)) for a in (2, 3) for part in parts]
         for a, part in products[:3]:
             prepare(a, part)
         flip_mask(0)
@@ -238,8 +239,9 @@ def tile_edgeencoder_b_kernel(
                 divide(n - 1)
             if n + 2 < BLOCKS:
                 flip_mask(n + 2)
-            if n + 3 < len(products):
-                prepare(*products[n + 3])
+            nth = 3 + 3 * (n // 4) + n % 4
+            if n % 4 != 3 and nth < len(products):
+                prepare(*products[nth])
             if n >= 6 and (n - 6) % 4 < 2:
                 context((n - 6) // 4, (n - 6) % 4)
             if n >= 28:

@@ -125,17 +125,17 @@ def tile_edgeencoder_b_kernel(
         y = held.tile([P, EMB_BLOCKS, EDGES], F32, name="y")
 
         def prepare(a, part):
+            j = part % HALVES
             acc = psum_a.tile([P, BANK], F32, name="acc")
-            if part in (3, 4):
-                j = part - 3
-                for b in range(BANK_BLOCKS):
-                    k = j * BANK_BLOCKS + b
-                    accumulate(nc, acc[:, block(b)], [(h[:, c, block(k)], wv_sb[:, c, block(a)]) for c in range(FEAT_BLOCKS)])
-                nc.scalar.copy(v_t[:, a, half(j)], acc[:])
-            else:
-                w_sb, dest, j = {0: (wk_sb, kk, 0), 1: (wk_sb, kk, 1), 2: (wq_sb, q, 0), 5: (wq_sb, q, 1)}[part]
+            if part < 2 * HALVES:
+                w_sb, dest = ((wk_sb, kk), (wq_sb, q))[part // HALVES]
                 accumulate(nc, acc[:], [(w_sb[:, c, block(a)], h[:, c, half(j)]) for c in range(FEAT_BLOCKS)])
-                nc.vector.tensor_copy(dest[:, a, half(j)], acc[:])
+                nc.scalar.copy(dest[:, a, half(j)], acc[:])
+            else:
+                for n in range(BANK_BLOCKS):
+                    k = j * BANK_BLOCKS + n
+                    accumulate(nc, acc[:, block(n)], [(h[:, c, block(k)], wv_sb[:, c, block(a)]) for c in range(FEAT_BLOCKS)])
+                nc.scalar.copy(v_t[:, a, half(j)], acc[:])
 
         def flip_mask(i):
             flipped = psum_t.tile([P, EDGES], BF16, name="flipped")
@@ -222,8 +222,7 @@ def tile_edgeencoder_b_kernel(
 
         for i in range(BLOCKS):
             nc.gpsimd.tensor_scalar(mask[:, i, :, :], adj_sb[:, i, :, :], -1.0, -MASKED, ALU.add, ALU.mult)
-        products = [(a, part) for a in (0, 1) for part in range(6)]
-        products += [(a, part) for parts in (range(3), range(3, 6)) for a in (2, 3) for part in parts]
+        products = [(a, part) for a in range(HEADS) for part in range(6)]
         for a, part in products[:3]:
             prepare(a, part)
         flip_mask(0)
@@ -239,9 +238,8 @@ def tile_edgeencoder_b_kernel(
                 divide(n - 1)
             if n + 2 < BLOCKS:
                 flip_mask(n + 2)
-            nth = 3 + 3 * (n // 4) + n % 4
-            if n % 4 != 3 and nth < len(products):
-                prepare(*products[nth])
+            if n + 3 < len(products):
+                prepare(*products[n + 3])
             if n >= 6 and (n - 6) % 4 < 2:
                 context((n - 6) // 4, (n - 6) % 4)
             if n >= 28:

@@ -56,12 +56,11 @@ def tile_edgeencoder_b_kernel(
     nc = tc.nc
     with (
         tc.tile_pool(name="held", bufs=1) as held,
-        tc.tile_pool(name="short", bufs=2) as short,
+        tc.tile_pool(name="short", bufs=3) as short,
         tc.tile_pool(name="work", bufs=3) as work,
         tc.tile_pool(name="stats", bufs=4) as stats,
-        tc.psum_pool(name="psum_s", bufs=3) as psum_s,
+        tc.psum_pool(name="psum_p", bufs=5) as psum_p,
         tc.psum_pool(name="psum_t", bufs=2) as psum_t,
-        tc.psum_pool(name="psum_a", bufs=2) as psum_a,
         tc.psum_pool(name="psum_c", bufs=1) as psum_c,
     ):
         offsets = held.tile([P, LIST // 16], U16, name="offsets")
@@ -76,7 +75,8 @@ def tile_edgeencoder_b_kernel(
         wo_sb = held.tile([P, FEAT_BLOCKS, FEAT], BF16, name="wo_sb")
         w1_sb = held.tile([P, FEAT_BLOCKS, EMB], BF16, name="w1_sb")
         w2_sb = held.tile([P, EMB_BLOCKS, EMB], BF16, name="w2_sb")
-        bias_row = held.tile([1, 2 * EMB], F32, name="bias_row")
+        b1_sb = held.tile([P, EMB_BLOCKS], F32, name="b1_sb")
+        b2_sb = held.tile([P, EMB_BLOCKS], F32, name="b2_sb")
         adj_sb = held.tile([P, BLOCKS, BLOCKS, P], F32, name="adj_sb")
         adj_by_key_block = adj.rearrange("(k p) e -> p k e", p=P)
 
@@ -90,19 +90,17 @@ def tile_edgeencoder_b_kernel(
         loads += [(wv_sb[:], rows_in_blocks(wv))]
         loads += [(adj_sb[:, i, :, :], adj_by_key_block[:, :, block(i)]) for i in range(2, BLOCKS)]
         loads += [(wo_sb[:], rows_in_blocks(wo)), (w1_sb[:], rows_in_blocks(w1)), (w2_sb[:], rows_in_blocks(w2))]
-        loads += [(bias_row[:, 0:EMB], b1.rearrange("r o -> o r")), (bias_row[:, EMB : 2 * EMB], b2.rearrange("r o -> o r"))]
+        loads += [(b1_sb[:], b1.rearrange("(r p) o -> p (r o)", p=P)), (b2_sb[:], b2.rearrange("(r p) o -> p (r o)", p=P))]
         for n, (sbuf_side, dram_side) in enumerate(loads):
             (nc.scalar, nc.sync)[n % 2].dma_start(sbuf_side, dram_side)
 
         ident = held.tile([P, P], BF16, name="ident")
         make_identity(nc, ident[:])
-        one = held.tile([1, 1], F32, name="one")
-        nc.vector.memset(one[:], 1.0)
 
         h = held.tile([P, FEAT_BLOCKS, EDGES], BF16, name="h")
         for m in range(FEAT_BLOCKS):
             for j in range(HALVES):
-                acc = psum_a.tile([P, BANK], F32, name="acc")
+                acc = psum_p.tile([P, BANK], F32, name="bank")
                 for end in range(2):
                     piece = end * HALVES + j
                     nc.tensor.matmul(
@@ -126,7 +124,7 @@ def tile_edgeencoder_b_kernel(
 
         def prepare(a, part):
             j = part % HALVES
-            acc = psum_a.tile([P, BANK], F32, name="acc")
+            acc = psum_p.tile([P, BANK], F32, name="bank")
             if part < 2 * HALVES:
                 w_sb, dest = ((wk_sb, kk), (wq_sb, q))[part // HALVES]
                 accumulate(nc, acc[:], [(w_sb[:, c, block(a)], h[:, c, half(j)]) for c in range(FEAT_BLOCKS)])
@@ -146,13 +144,14 @@ def tile_edgeencoder_b_kernel(
         groups = [(0, 0), (0, 1), (1, 0), (1, 1), (2, 0), (3, 0), (2, 1), (3, 1)]
         blocks = [(a, j * BANK_BLOCKS + b) for a, j in groups for b in range(BANK_BLOCKS)]
         s_of, z_of, num_of, den_of, att_of = {}, {}, {}, {}, {}
-        att_t_of, ctx_of = {}, {}
+        att_t_of = {}
+        ctx_of = {}
 
         def scores(n):
             a, i = blocks[n]
             s_of[n] = []
             for t in range(HALVES):
-                s = psum_s.tile([P, BANK], F32, name="s")
+                s = psum_p.tile([P, BANK], F32, name="bank")
                 nc.tensor.matmul(s[:], q[:, a, block(i)], kk[:, a, half(t)], start=True, stop=True)
                 s_of[n].append(s)
 
@@ -178,46 +177,45 @@ def tile_edgeencoder_b_kernel(
             nc.gpsimd.tensor_scalar(att_of[n][:], num_of[n][:], rden[:], 0.0, ALU.mult, ALU.add)
 
         def flip_weights(n):
-            group, b = divmod(n, BANK_BLOCKS)
-            if b == 0:
-                att_t_of[group] = work.tile([P, BLOCKS, BANK], BF16, name="att_t")
             flipped = psum_t.tile([P, EDGES], BF16, name="flipped")
             for k in range(BLOCKS):
                 nc.tensor.transpose(flipped[:, block(k)], att_of[n][:, block(k)], ident[:])
-            nc.scalar.copy(att_t_of[group][:, :, block(b)], flipped[:].rearrange("p (k e) -> p k e", k=BLOCKS))
+            att_t_of[n] = work.tile([P, EDGES], BF16, name="att_t")
+            if n % 4 == 0:
+                nc.vector.tensor_copy(att_t_of[n][:], flipped[:])
+            else:
+                nc.scalar.copy(att_t_of[n][:], flipped[:])
 
-        def context(group, part):
+        def context(n):
+            group, b = divmod(n, BANK_BLOCKS)
             a, j = groups[group]
-            if part == 0:
+            if b == 0:
                 ctx_of[group] = psum_c.tile([P, BANK], F32, name="ctx_ps")
-            keys = range(part * BANK_BLOCKS, (part + 1) * BANK_BLOCKS)
-            accumulate(
-                nc,
-                ctx_of[group][:],
-                [(v_t[:, a, block(k)], att_t_of[group][:, k, :]) for k in keys],
-                start=(part == 0),
-                stop=(part == 1),
-            )
-            if part == 1:
+            accumulate(nc, ctx_of[group][:, block(b)], [(v_t[:, a, block(k)], att_t_of[n][:, block(k)]) for k in range(BLOCKS)])
+            if b == BANK_BLOCKS - 1:
                 nc.scalar.copy(ctx[:, a, half(j)], ctx_of[group][:])
 
-        def edge_out(j, m):
-            acc = psum_a.tile([P, BANK], F32, name="acc")
-            accumulate(nc, acc[:], [(wo_sb[:, a, block(m)], ctx[:, a, half(j)]) for a in range(HEADS)])
-            if m % 2 == 0:
-                nc.scalar.copy(eo[:, m, half(j)], acc[:])
-            else:
-                nc.vector.tensor_copy(eo[:, m, half(j)], acc[:])
+        eo_of = {}
+
+        def edge_out(j, m, heads):
+            first, last = heads[0] == 0, heads[-1] == HEADS - 1
+            if first:
+                eo_of[j, m] = psum_p.tile([P, BANK], F32, name="bank")
+            accumulate(nc, eo_of[j, m][:], [(wo_sb[:, a, block(m)], ctx[:, a, half(j)]) for a in heads], start=first, stop=last)
+            if last and m % 2 == 0:
+                nc.scalar.copy(eo[:, m, half(j)], eo_of[j, m][:])
+            elif last:
+                nc.vector.tensor_copy(eo[:, m, half(j)], eo_of[j, m][:])
 
         def hidden(j, r):
-            acc = psum_a.tile([P, BANK], F32, name="acc")
+            acc = psum_p.tile([P, BANK], F32, name="bank")
             accumulate(nc, acc[:], [(w1_sb[:, c, block(r)], eo[:, c, half(j)]) for c in range(FEAT_BLOCKS)])
-            nc.scalar.activation(x[:, r, half(j)], acc[:], ACT.Gelu_apprx_tanh, bias=bias[:, r : r + 1])
+            nc.scalar.activation(x[:, r, half(j)], acc[:], ACT.Gelu_apprx_tanh, bias=b1_sb[:, r : r + 1])
 
         def embed(j, r):
-            acc = psum_a.tile([P, BANK], F32, name="acc")
+            acc = psum_p.tile([P, BANK], F32, name="bank")
             accumulate(nc, acc[:], [(w2_sb[:, c, block(r)], x[:, c, half(j)]) for c in range(EMB_BLOCKS)])
-            nc.vector.tensor_scalar_add(y[:, r, half(j)], acc[:], bias[:, EMB_BLOCKS + r : EMB_BLOCKS + r + 1])
+            nc.vector.tensor_scalar_add(y[:, r, half(j)], acc[:], b2_sb[:, r : r + 1])
             nc.sync.dma_start(out[block(r), half(j)], y[:, r, half(j)])
 
         for i in range(BLOCKS):
@@ -229,42 +227,42 @@ def tile_edgeencoder_b_kernel(
         scores(0)
         flip_mask(1)
 
-        for n in range(len(blocks)):
-            scale_and_mask(n)
-            if n + 1 < len(blocks):
+        all_heads = list(range(HEADS))
+
+        def in_loop(n):
+            return 0 <= n < len(blocks)
+
+        for n in range(len(blocks) + 4):
+            if in_loop(n):
+                scale_and_mask(n)
+            if in_loop(n + 1):
                 scores(n + 1)
-            exponentials(n)
-            if n >= 1:
-                divide(n - 1)
+            if in_loop(n - 1):
+                exponentials(n - 1)
+            if in_loop(n - 2):
+                divide(n - 2)
             if n + 2 < BLOCKS:
                 flip_mask(n + 2)
             if n + 3 < len(products):
                 prepare(*products[n + 3])
-            if n >= 6 and (n - 6) % 4 < 2:
-                context((n - 6) // 4, (n - 6) % 4)
-            if n >= 28:
-                edge_out(0, n - 28)
-            if n >= 2:
-                flip_weights(n - 2)
+            if 28 <= n < 28 + FEAT_BLOCKS:
+                edge_out(0, n - 28, all_heads)
+            if in_loop(n - 3):
+                flip_weights(n - 3)
+            if in_loop(n - 4):
+                context(n - 4)
+            if n == len(blocks):
+                for m in range(FEAT_BLOCKS):
+                    edge_out(1, m, all_heads[:-1])
+            if n == len(blocks) + 1:
+                for r in range(EMB_BLOCKS):
+                    hidden(0, r)
+            if n == len(blocks) + 2:
+                for r in range(EMB_BLOCKS):
+                    embed(0, r)
 
-        divide(len(blocks) - 1)
-        flip_weights(len(blocks) - 2)
-        flip_weights(len(blocks) - 1)
-
-        bias_ps = psum_a.tile([P, 2 * EMB_BLOCKS], F32, name="acc")
-        for n in range(2 * EMB_BLOCKS):
-            nc.tensor.matmul(bias_ps[:, n : n + 1], bias_row[:, block(n)], one[:], start=True, stop=True)
-        bias = held.tile([P, 2 * EMB_BLOCKS], F32, name="bias")
-        nc.vector.tensor_copy(bias[:], bias_ps[:])
-
-        for r in range(EMB_BLOCKS):
-            hidden(0, r)
-        for part in range(2):
-            context(len(groups) - 1, part)
-        for r in range(EMB_BLOCKS):
-            embed(0, r)
         for m in range(FEAT_BLOCKS):
-            edge_out(1, m)
+            edge_out(1, m, all_heads[-1:])
         for r in range(EMB_BLOCKS):
             hidden(1, r)
         for r in range(EMB_BLOCKS):

@@ -181,10 +181,7 @@ def tile_edgeencoder_b_kernel(
             for k in range(BLOCKS):
                 nc.tensor.transpose(flipped[:, block(k)], att_of[n][:, block(k)], ident[:])
             att_t_of[n] = work.tile([P, EDGES], BF16, name="att_t")
-            if n % 4 == 0:
-                nc.vector.tensor_copy(att_t_of[n][:], flipped[:])
-            else:
-                nc.scalar.copy(att_t_of[n][:], flipped[:])
+            nc.scalar.copy(att_t_of[n][:], flipped[:])
 
         def context(n):
             group, b = divmod(n, BANK_BLOCKS)

@@ -96,6 +96,8 @@ def tile_edgeencoder_b_kernel(
 
         ident = held.tile([P, P], BF16, name="ident")
         make_identity(nc, ident[:])
+        minus_one = held.tile([P, 1], F32, name="minus_one")
+        nc.vector.memset(minus_one[:], -1.0)
 
         h = held.tile([P, FEAT_BLOCKS, EDGES], BF16, name="h")
         for m in range(FEAT_BLOCKS):
@@ -139,7 +141,7 @@ def tile_edgeencoder_b_kernel(
             flipped = psum_t.tile([P, EDGES], BF16, name="flipped")
             for k in range(BLOCKS):
                 nc.tensor.transpose(flipped[:, block(k)], mask[:, i, k, :], ident[:])
-            nc.vector.tensor_copy(mask_t[:, i, :], flipped[:])
+            nc.scalar.copy(mask_t[:, i, :], flipped[:])
 
         groups = [(0, 0), (0, 1), (1, 0), (1, 1), (2, 0), (3, 0), (2, 1), (3, 1)]
         blocks = [(a, j * BANK_BLOCKS + b) for a, j in groups for b in range(BANK_BLOCKS)]
@@ -172,7 +174,7 @@ def tile_edgeencoder_b_kernel(
 
         def divide(n):
             rden = stats.tile([P, 1], F32, name="rden")
-            nc.vector.reciprocal(rden[:], den_of[n][:])
+            nc.gpsimd.tensor_tensor(rden[:], den_of[n][:], minus_one[:], ALU.pow)
             att_of[n] = work.tile([P, EDGES], BF16, name="att")
             nc.gpsimd.tensor_scalar(att_of[n][:], num_of[n][:], rden[:], 0.0, ALU.mult, ALU.add)
 

@@ -232,12 +232,12 @@ def tile_edgeencoder_b_kernel(
             return 0 <= n < len(blocks)
 
         for n in range(len(blocks) + 4):
+            if in_loop(n - 1):
+                exponentials(n - 1)
             if in_loop(n):
                 scale_and_mask(n)
             if in_loop(n + 1):
                 scores(n + 1)
-            if in_loop(n - 1):
-                exponentials(n - 1)
             if in_loop(n - 2):
                 divide(n - 2)
             if n + 2 < BLOCKS:

@@ -124,13 +124,13 @@ def tile_edgeencoder_b_kernel(
         x = held.tile([P, EMB_BLOCKS, EDGES], BF16, name="x")
         y = held.tile([P, EMB_BLOCKS, EDGES], F32, name="y")
 
-        def prepare(a, part):
+        def prepare(a, part, copy=nc.scalar.copy):
             j = part % HALVES
             acc = psum_p.tile([P, BANK], F32, name="bank")
             if part < 2 * HALVES:
                 w_sb, dest = ((wk_sb, kk), (wq_sb, q))[part // HALVES]
                 accumulate(nc, acc[:], [(w_sb[:, c, block(a)], h[:, c, half(j)]) for c in range(FEAT_BLOCKS)])
-                nc.scalar.copy(dest[:, a, half(j)], acc[:])
+                copy(dest[:, a, half(j)], acc[:])
             else:
                 for n in range(BANK_BLOCKS):
                     k = j * BANK_BLOCKS + n
@@ -174,16 +174,23 @@ def tile_edgeencoder_b_kernel(
 
         def divide(n):
             rden = stats.tile([P, 1], F32, name="rden")
-            nc.gpsimd.tensor_tensor(rden[:], den_of[n][:], minus_one[:], ALU.pow)
             att_of[n] = work.tile([P, EDGES], BF16, name="att")
-            nc.gpsimd.tensor_scalar(att_of[n][:], num_of[n][:], rden[:], 0.0, ALU.mult, ALU.add)
+            if n + 2 < len(blocks):
+                nc.gpsimd.tensor_tensor(rden[:], den_of[n][:], minus_one[:], ALU.pow)
+                nc.gpsimd.tensor_scalar(att_of[n][:], num_of[n][:], rden[:], 0.0, ALU.mult, ALU.add)
+            else:
+                nc.vector.reciprocal(rden[:], den_of[n][:])
+                nc.vector.tensor_scalar(att_of[n][:], num_of[n][:], rden[:], None, ALU.mult)
 
         def flip_weights(n):
             flipped = psum_t.tile([P, EDGES], BF16, name="flipped")
             for k in range(BLOCKS):
                 nc.tensor.transpose(flipped[:, block(k)], att_of[n][:, block(k)], ident[:])
             att_t_of[n] = work.tile([P, EDGES], BF16, name="att_t")
-            nc.scalar.copy(att_t_of[n][:], flipped[:])
+            if n + 3 < len(blocks):
+                nc.scalar.copy(att_t_of[n][:], flipped[:])
+            else:
+                nc.vector.tensor_copy(att_t_of[n][:], flipped[:])
 
         def context(n):
             group, b = divmod(n, BANK_BLOCKS)
@@ -191,8 +198,10 @@ def tile_edgeencoder_b_kernel(
             if b == 0:
                 ctx_of[group] = psum_c.tile([P, BANK], F32, name="ctx_ps")
             accumulate(nc, ctx_of[group][:, block(b)], [(v_t[:, a, block(k)], att_t_of[n][:, block(k)]) for k in range(BLOCKS)])
-            if b == BANK_BLOCKS - 1:
+            if b == BANK_BLOCKS - 1 and group < len(groups) - 1:
                 nc.scalar.copy(ctx[:, a, half(j)], ctx_of[group][:])
+            elif b == BANK_BLOCKS - 1:
+                nc.vector.tensor_copy(ctx[:, a, half(j)], ctx_of[group][:])
 
         eo_of = {}
 
@@ -220,8 +229,9 @@ def tile_edgeencoder_b_kernel(
         for i in range(BLOCKS):
             nc.gpsimd.tensor_scalar(mask[:, i, :, :], adj_sb[:, i, :, :], -1.0, -MASKED, ALU.add, ALU.mult)
         products = [(a, part) for a in range(HEADS) for part in range(6)]
-        for a, part in products[:3]:
-            prepare(a, part)
+        prepare(0, 0, nc.vector.tensor_copy)
+        prepare(0, 2)
+        prepare(0, 1, nc.vector.tensor_copy)
         flip_mask(0)
         scores(0)
         flip_mask(1)

@@ -198,10 +198,10 @@ def tile_edgeencoder_b_kernel(
             if b == 0:
                 ctx_of[group] = psum_c.tile([P, BANK], F32, name="ctx_ps")
             accumulate(nc, ctx_of[group][:, block(b)], [(v_t[:, a, block(k)], att_t_of[n][:, block(k)]) for k in range(BLOCKS)])
-            if b == BANK_BLOCKS - 1 and group < len(groups) - 1:
-                nc.scalar.copy(ctx[:, a, half(j)], ctx_of[group][:])
+            if group == len(groups) - 1:
+                nc.vector.tensor_copy(ctx[:, a, block(blocks[n][1])], ctx_of[group][:, block(b)])
             elif b == BANK_BLOCKS - 1:
-                nc.vector.tensor_copy(ctx[:, a, half(j)], ctx_of[group][:])
+                nc.scalar.copy(ctx[:, a, half(j)], ctx_of[group][:])
 
         eo_of = {}
 
@@ -210,21 +210,28 @@ def tile_edgeencoder_b_kernel(
             if first:
                 eo_of[j, m] = psum_p.tile([P, BANK], F32, name="bank")
             accumulate(nc, eo_of[j, m][:], [(wo_sb[:, a, block(m)], ctx[:, a, half(j)]) for a in heads], start=first, stop=last)
-            if last and m % 2 == 0:
-                nc.scalar.copy(eo[:, m, half(j)], eo_of[j, m][:])
-            elif last:
-                nc.vector.tensor_copy(eo[:, m, half(j)], eo_of[j, m][:])
 
-        def hidden(j, r):
-            acc = psum_p.tile([P, BANK], F32, name="bank")
-            accumulate(nc, acc[:], [(w1_sb[:, c, block(r)], eo[:, c, half(j)]) for c in range(FEAT_BLOCKS)])
-            nc.scalar.activation(x[:, r, half(j)], acc[:], ACT.Gelu_apprx_tanh, bias=b1_sb[:, r : r + 1])
+        def edge_out_leaves(j, m, cols):
+            in_bank = eo_of[j, m][:, cols.start - j * BANK : cols.stop - j * BANK]
+            if m % 2 == 0:
+                nc.scalar.copy(eo[:, m, cols], in_bank)
+            else:
+                nc.vector.tensor_copy(eo[:, m, cols], in_bank)
 
-        def embed(j, r):
+        def bank_for(cols):
             acc = psum_p.tile([P, BANK], F32, name="bank")
-            accumulate(nc, acc[:], [(w2_sb[:, c, block(r)], x[:, c, half(j)]) for c in range(EMB_BLOCKS)])
-            nc.vector.tensor_scalar_add(y[:, r, half(j)], acc[:], b2_sb[:, r : r + 1])
-            nc.sync.dma_start(out[block(r), half(j)], y[:, r, half(j)])
+            return acc[:, 0 : cols.stop - cols.start]
+
+        def hidden(cols, r):
+            acc = bank_for(cols)
+            accumulate(nc, acc, [(w1_sb[:, c, block(r)], eo[:, c, cols]) for c in range(FEAT_BLOCKS)])
+            nc.scalar.activation(x[:, r, cols], acc, ACT.Gelu_apprx_tanh, bias=b1_sb[:, r : r + 1])
+
+        def embed(cols, r):
+            acc = bank_for(cols)
+            accumulate(nc, acc, [(w2_sb[:, c, block(r)], x[:, c, cols]) for c in range(EMB_BLOCKS)])
+            nc.vector.tensor_scalar_add(y[:, r, cols], acc, b2_sb[:, r : r + 1])
+            nc.sync.dma_start(out[block(r), cols], y[:, r, cols])
 
         for i in range(BLOCKS):
             nc.gpsimd.tensor_scalar(mask[:, i, :, :], adj_sb[:, i, :, :], -1.0, -MASKED, ALU.add, ALU.mult)
@@ -256,6 +263,7 @@ def tile_edgeencoder_b_kernel(
                 prepare(*products[n + 3])
             if 28 <= n < 28 + FEAT_BLOCKS:
                 edge_out(0, n - 28, all_heads)
+                edge_out_leaves(0, n - 28, half(0))
             if in_loop(n - 3):
                 flip_weights(n - 3)
             if in_loop(n - 4):
@@ -265,14 +273,20 @@ def tile_edgeencoder_b_kernel(
                     edge_out(1, m, all_heads[:-1])
             if n == len(blocks) + 1:
                 for r in range(EMB_BLOCKS):
-                    hidden(0, r)
+                    hidden(half(0), r)
             if n == len(blocks) + 2:
                 for r in range(EMB_BLOCKS):
-                    embed(0, r)
+                    embed(half(0), r)
 
         for m in range(FEAT_BLOCKS):
             edge_out(1, m, all_heads[-1:])
-        for r in range(EMB_BLOCKS):
-            hidden(1, r)
-        for r in range(EMB_BLOCKS):
-            embed(1, r)
+        pieces = [slice(BANK, BANK + BANK // 2), slice(BANK + BANK // 2, EDGES)]
+        for cols in pieces:
+            for m in range(FEAT_BLOCKS):
+                edge_out_leaves(1, m, cols)
+        for cols in pieces:
+            for r in range(EMB_BLOCKS):
+                hidden(cols, r)
+        for cols in pieces:
+            for r in range(EMB_BLOCKS):
+                embed(cols, r)

@@ -92,7 +92,8 @@ def tile_edgeencoder_b_kernel(
         loads += [(wo_sb[:], rows_in_blocks(wo)), (w1_sb[:], rows_in_blocks(w1)), (w2_sb[:], rows_in_blocks(w2))]
         loads += [(b1_sb[:], b1.rearrange("(r p) o -> p (r o)", p=P)), (b2_sb[:], b2.rearrange("(r p) o -> p (r o)", p=P))]
         for n, (sbuf_side, dram_side) in enumerate(loads):
-            (nc.scalar, nc.sync)[n % 2].dma_start(sbuf_side, dram_side)
+            queue = nc.scalar if n < 2 + FEAT_BLOCKS and n % 2 == 0 else nc.sync
+            queue.dma_start(sbuf_side, dram_side)
 
         ident = held.tile([P, P], BF16, name="ident")
         make_identity(nc, ident[:])

@@ -99,6 +99,8 @@ def tile_edgeencoder_b_kernel(
         make_identity(nc, ident[:])
         minus_one = held.tile([P, 1], F32, name="minus_one")
         nc.vector.memset(minus_one[:], -1.0)
+        warm_up = held.tile([P, 1], F32, name="warm_up")
+        nc.scalar.activation(warm_up[:], minus_one[:], ACT.Exp)
 
         h = held.tile([P, FEAT_BLOCKS, EDGES], BF16, name="h")
         for m in range(FEAT_BLOCKS):

import math

import concourse.mybir as mybir
from concourse.masks import make_identity

BF16 = mybir.dt.bfloat16
F32 = mybir.dt.float32
U16 = mybir.dt.uint16
ALU = mybir.AluOpType
ACT = mybir.ActivationFunctionType
AXIS = mybir.AxisListType

P = 128
NODES = 1024
EDGES = 1024
LIST = 2 * EDGES
FEAT = 512
HEADS = 4
EMB = 256
BANK = 512
BANK_OFFS = BANK // 16
BANK_BLOCKS = BANK // P
HALVES = EDGES // BANK
BLOCKS = EDGES // P
FEAT_BLOCKS = FEAT // P
EMB_BLOCKS = EMB // P
SCALE = 1.0 / math.sqrt(P)
MASKED = -1.0e9

FLOPS = 2 * (
    P * FEAT * LIST
    + 3 * FEAT * FEAT * EDGES
    + 2 * FEAT * EDGES * EDGES
    + FEAT * FEAT * EDGES
    + FEAT * EMB * EDGES
    + EMB * EMB * EDGES
)


def block(n):
    return slice(n * P, (n + 1) * P)


def half(n):
    return slice(n * BANK, (n + 1) * BANK)


def accumulate(nc, acc, pairs, start=True, stop=True):
    for n, (lhsT, rhs) in enumerate(pairs):
        nc.tensor.matmul(acc, lhsT, rhs, start=(start and n == 0), stop=(stop and n == len(pairs) - 1))


def tile_edgeencoder_b_kernel(
    tc, table, wn, edge_feats, wq, wk, wv, wo, w1, b1, w2, b2, adj, offs, out
):
    nc = tc.nc
    with (
        tc.tile_pool(name="held", bufs=1) as held,
        tc.tile_pool(name="short", bufs=3) as short,
        tc.tile_pool(name="work", bufs=3) as work,
        tc.tile_pool(name="stats", bufs=4) as stats,
        tc.psum_pool(name="psum_p", bufs=5) as psum_p,
        tc.psum_pool(name="psum_t", bufs=2) as psum_t,
        tc.psum_pool(name="psum_c", bufs=1) as psum_c,
    ):
        offsets = held.tile([P, LIST // 16], U16, name="offsets")
        nc.sync.dma_start(offsets[:], offs)

        nodes = held.tile([P, NODES], BF16, name="nodes")
        wn_sb = held.tile([P, FEAT], BF16, name="wn_sb")
        feats = held.tile([P, FEAT_BLOCKS, EDGES], F32, name="feats")
        wk_sb = held.tile([P, FEAT_BLOCKS, FEAT], BF16, name="wk_sb")
        wq_sb = held.tile([P, FEAT_BLOCKS, FEAT], BF16, name="wq_sb")
        wv_sb = held.tile([P, FEAT_BLOCKS, FEAT], BF16, name="wv_sb")
        wo_sb = held.tile([P, FEAT_BLOCKS, FEAT], BF16, name="wo_sb")
        w1_sb = held.tile([P, FEAT_BLOCKS, EMB], BF16, name="w1_sb")
        w2_sb = held.tile([P, EMB_BLOCKS, EMB], BF16, name="w2_sb")
        b1_sb = held.tile([P, EMB_BLOCKS], F32, name="b1_sb")
        b2_sb = held.tile([P, EMB_BLOCKS], F32, name="b2_sb")
        adj_sb = held.tile([P, BLOCKS, BLOCKS, P], F32, name="adj_sb")
        adj_by_key_block = adj.rearrange("(k p) e -> p k e", p=P)

        def rows_in_blocks(w):
            return w.rearrange("(c p) m -> p c m", p=P)

        loads = [(nodes[:], table), (wn_sb[:], wn)]
        loads += [(feats[:, m, :], edge_feats[block(m), :]) for m in range(FEAT_BLOCKS)]
        loads += [(wk_sb[:], rows_in_blocks(wk)), (wq_sb[:], rows_in_blocks(wq))]
        loads += [(adj_sb[:, i, :, :], adj_by_key_block[:, :, block(i)]) for i in range(2)]
        loads += [(wv_sb[:], rows_in_blocks(wv))]
        loads += [(adj_sb[:, i, :, :], adj_by_key_block[:, :, block(i)]) for i in range(2, BLOCKS)]
        loads += [(wo_sb[:], rows_in_blocks(wo)), (w1_sb[:], rows_in_blocks(w1)), (w2_sb[:], rows_in_blocks(w2))]
        loads += [(b1_sb[:], b1.rearrange("(r p) o -> p (r o)", p=P)), (b2_sb[:], b2.rearrange("(r p) o -> p (r o)", p=P))]
        for n, (sbuf_side, dram_side) in enumerate(loads):
            queue = nc.scalar if n < 2 + FEAT_BLOCKS and n % 2 == 0 else nc.sync
            queue.dma_start(sbuf_side, dram_side)

        ident = held.tile([P, P], BF16, name="ident")
        make_identity(nc, ident[:])
        minus_one = held.tile([P, 1], F32, name="minus_one")
        nc.vector.memset(minus_one[:], -1.0)
        warm_up = held.tile([P, 1], F32, name="warm_up")
        nc.scalar.activation(warm_up[:], minus_one[:], ACT.Exp)

        h = held.tile([P, FEAT_BLOCKS, EDGES], BF16, name="h")
        for m in range(FEAT_BLOCKS):
            for j in range(HALVES):
                acc = psum_p.tile([P, BANK], F32, name="bank")
                for end in range(2):
                    piece = end * HALVES + j
                    nc.tensor.matmul(
                        acc[:],
                        wn_sb[:, block(m)],
                        nodes[:].indirect(offsets[:, piece * BANK_OFFS : (piece + 1) * BANK_OFFS]),
                        start=(end == 0),
                        stop=(end == 1),
                    )
                nc.vector.tensor_tensor(h[:, m, half(j)], acc[:], feats[:, m, half(j)], ALU.add)

        q = held.tile([P, HEADS, EDGES], BF16, name="q")
        kk = held.tile([P, HEADS, EDGES], BF16, name="kk")
        v_t = held.tile([P, HEADS, EDGES], BF16, name="v_t")
        mask = held.tile([P, BLOCKS, BLOCKS, P], BF16, name="mask")
        mask_t = held.tile([P, BLOCKS, EDGES], BF16, name="mask_t")
        ctx = held.tile([P, HEADS, EDGES], BF16, name="ctx")
        eo = held.tile([P, FEAT_BLOCKS, EDGES], BF16, name="eo")
        x = held.tile([P, EMB_BLOCKS, EDGES], BF16, name="x")
        y = held.tile([P, EMB_BLOCKS, EDGES], F32, name="y")

        def prepare(a, part, copy=nc.scalar.copy):
            j = part % HALVES
            acc = psum_p.tile([P, BANK], F32, name="bank")
            if part < 2 * HALVES:
                w_sb, dest = ((wk_sb, kk), (wq_sb, q))[part // HALVES]
                accumulate(nc, acc[:], [(w_sb[:, c, block(a)], h[:, c, half(j)]) for c in range(FEAT_BLOCKS)])
                copy(dest[:, a, half(j)], acc[:])
            else:
                for n in range(BANK_BLOCKS):
                    k = j * BANK_BLOCKS + n
                    accumulate(nc, acc[:, block(n)], [(h[:, c, block(k)], wv_sb[:, c, block(a)]) for c in range(FEAT_BLOCKS)])
                nc.scalar.copy(v_t[:, a, half(j)], acc[:])

        def flip_mask(i):
            flipped = psum_t.tile([P, EDGES], BF16, name="flipped")
            for k in range(BLOCKS):
                nc.tensor.transpose(flipped[:, block(k)], mask[:, i, k, :], ident[:])
            nc.scalar.copy(mask_t[:, i, :], flipped[:])

        groups = [(0, 0), (0, 1), (1, 0), (1, 1), (2, 0), (3, 0), (2, 1), (3, 1)]
        blocks = [(a, j * BANK_BLOCKS + b) for a, j in groups for b in range(BANK_BLOCKS)]
        s_of, z_of, num_of, den_of, att_of = {}, {}, {}, {}, {}
        att_t_of = {}
        ctx_of = {}

        def scores(n):
            a, i = blocks[n]
            s_of[n] = []
            for t in range(HALVES):
                s = psum_p.tile([P, BANK], F32, name="bank")
                nc.tensor.matmul(s[:], q[:, a, block(i)], kk[:, a, half(t)], start=True, stop=True)
                s_of[n].append(s)

        def scale_and_mask(n):
            i = blocks[n][1]
            z_of[n] = short.tile([P, EDGES], F32, name="z")
            for t in range(HALVES):
                nc.vector.scalar_tensor_tensor(
                    z_of[n][:, half(t)], s_of[n][t][:], SCALE, mask_t[:, i, half(t)], ALU.mult, ALU.add
                )

        def exponentials(n):
            neg_max = stats.tile([P, 1], F32, name="neg_max")
            nc.vector.tensor_reduce(neg_max[:], z_of[n][:], AXIS.X, ALU.max, negate=True)
            num_of[n] = work.tile([P, EDGES], F32, name="num")
            den_of[n] = stats.tile([P, 1], F32, name="den")
            nc.scalar.activation(num_of[n][:], z_of[n][:], ACT.Exp, bias=neg_max[:], accum_out=den_of[n][:])

        def divide(n):
            rden = stats.tile([P, 1], F32, name="rden")
            att_of[n] = work.tile([P, EDGES], BF16, name="att")
            if n + 2 < len(blocks):
                nc.gpsimd.tensor_tensor(rden[:], den_of[n][:], minus_one[:], ALU.pow)
                nc.gpsimd.tensor_scalar(att_of[n][:], num_of[n][:], rden[:], 0.0, ALU.mult, ALU.add)
            else:
                nc.vector.reciprocal(rden[:], den_of[n][:])
                nc.vector.tensor_scalar(att_of[n][:], num_of[n][:], rden[:], None, ALU.mult)

        def flip_weights(n):
            flipped = psum_t.tile([P, EDGES], BF16, name="flipped")
            for k in range(BLOCKS):
                nc.tensor.transpose(flipped[:, block(k)], att_of[n][:, block(k)], ident[:])
            att_t_of[n] = work.tile([P, EDGES], BF16, name="att_t")
            if n + 3 < len(blocks):
                nc.scalar.copy(att_t_of[n][:], flipped[:])
            else:
                nc.vector.tensor_copy(att_t_of[n][:], flipped[:])

        def context(n):
            group, b = divmod(n, BANK_BLOCKS)
            a, j = groups[group]
            if b == 0:
                ctx_of[group] = psum_c.tile([P, BANK], F32, name="ctx_ps")
            accumulate(nc, ctx_of[group][:, block(b)], [(v_t[:, a, block(k)], att_t_of[n][:, block(k)]) for k in range(BLOCKS)])
            if group == len(groups) - 1:
                nc.vector.tensor_copy(ctx[:, a, block(blocks[n][1])], ctx_of[group][:, block(b)])
            elif b == BANK_BLOCKS - 1:
                nc.scalar.copy(ctx[:, a, half(j)], ctx_of[group][:])

        eo_of = {}

        def edge_out(j, m, heads):
            first, last = heads[0] == 0, heads[-1] == HEADS - 1
            if first:
                eo_of[j, m] = psum_p.tile([P, BANK], F32, name="bank")
            accumulate(nc, eo_of[j, m][:], [(wo_sb[:, a, block(m)], ctx[:, a, half(j)]) for a in heads], start=first, stop=last)

        def edge_out_leaves(j, m, cols):
            in_bank = eo_of[j, m][:, cols.start - j * BANK : cols.stop - j * BANK]
            if m % 2 == 0:
                nc.scalar.copy(eo[:, m, cols], in_bank)
            else:
                nc.vector.tensor_copy(eo[:, m, cols], in_bank)

        def bank_for(cols):
            acc = psum_p.tile([P, BANK], F32, name="bank")
            return acc[:, 0 : cols.stop - cols.start]

        def hidden(cols, r):
            acc = bank_for(cols)
            accumulate(nc, acc, [(w1_sb[:, c, block(r)], eo[:, c, cols]) for c in range(FEAT_BLOCKS)])
            nc.scalar.activation(x[:, r, cols], acc, ACT.Gelu_apprx_tanh, bias=b1_sb[:, r : r + 1])

        def embed(cols, r):
            acc = bank_for(cols)
            accumulate(nc, acc, [(w2_sb[:, c, block(r)], x[:, c, cols]) for c in range(EMB_BLOCKS)])
            nc.vector.tensor_scalar_add(y[:, r, cols], acc, b2_sb[:, r : r + 1])
            nc.sync.dma_start(out[block(r), cols], y[:, r, cols])

        for i in range(BLOCKS):
            nc.gpsimd.tensor_scalar(mask[:, i, :, :], adj_sb[:, i, :, :], -1.0, -MASKED, ALU.add, ALU.mult)
        products = [(a, part) for a in range(HEADS) for part in range(6)]
        prepare(0, 0, nc.vector.tensor_copy)
        prepare(0, 2)
        prepare(0, 1, nc.vector.tensor_copy)
        flip_mask(0)
        scores(0)
        flip_mask(1)

        all_heads = list(range(HEADS))

        def in_loop(n):
            return 0 <= n < len(blocks)

        for n in range(len(blocks) + 4):
            if in_loop(n - 1):
                exponentials(n - 1)
            if in_loop(n):
                scale_and_mask(n)
            if in_loop(n + 1):
                scores(n + 1)
            if in_loop(n - 2):
                divide(n - 2)
            if n + 2 < BLOCKS:
                flip_mask(n + 2)
            if n + 3 < len(products):
                prepare(*products[n + 3])
            if 28 <= n < 28 + FEAT_BLOCKS:
                edge_out(0, n - 28, all_heads)
                edge_out_leaves(0, n - 28, half(0))
            if in_loop(n - 3):
                flip_weights(n - 3)
            if in_loop(n - 4):
                context(n - 4)
            if n == len(blocks):
                for m in range(FEAT_BLOCKS):
                    edge_out(1, m, all_heads[:-1])
            if n == len(blocks) + 1:
                for r in range(EMB_BLOCKS):
                    hidden(half(0), r)
            if n == len(blocks) + 2:
                for r in range(EMB_BLOCKS):
                    embed(half(0), r)

        for m in range(FEAT_BLOCKS):
            edge_out(1, m, all_heads[-1:])
        pieces = [slice(BANK, BANK + BANK // 2), slice(BANK + BANK // 2, EDGES)]
        for cols in pieces:
            for m in range(FEAT_BLOCKS):
                edge_out_leaves(1, m, cols)
        for cols in pieces:
            for r in range(EMB_BLOCKS):
                hidden(cols, r)
        for cols in pieces:
            for r in range(EMB_BLOCKS):
                embed(cols, r)
